import numpy as np
import ml_dtypes


BF16 = ml_dtypes.bfloat16


def bf(x):
    return np.asarray(x, np.float32).astype(BF16)


def f64(x):
    return np.asarray(x).astype(np.float64)


E2M1 = np.array([0.0, 0.5, 1.0, 1.5, 2.0, 3.0, 4.0, 6.0, -0.0, -0.5, -1.0, -1.5, -2.0, -3.0, -4.0, -6.0])


def pack_weight(w, fmt):
    k, n = w.shape
    w = f64(bf(w)).reshape(k // 32, 32, n)
    amax = np.abs(w).max(1)
    if fmt == "e4m3":
        byte = np.frexp(amax)[1] - 1 + 127 - 7
    else:
        mant, ex = np.frexp(amax / 6.0)
        byte = np.where(mant > 0.5, ex, ex - 1) + 127
    byte = np.clip(np.where(amax > 0, byte, 1), 1, 254)
    scaled = (w * np.exp2(127.0 - byte)[:, None, :]).reshape(k, n).astype(np.float32)
    by_word = np.ascontiguousarray(scaled.reshape(k // 512, 128, 4, n).transpose(0, 1, 3, 2))
    if fmt == "e4m3":
        words = by_word.astype(ml_dtypes.float8_e4m3fn).view(np.uint8)
    else:
        c = by_word.astype(ml_dtypes.float4_e2m1fn).view(np.uint8) & 0xF
        words = c[..., 0::2] | (c[..., 1::2] << 4)
    return np.ascontiguousarray(words), np.ascontiguousarray(byte.astype(np.uint8).reshape(k // 512, 16, n))


def unpack_weight(words, scales, fmt):
    g, p, n, _ = words.shape
    if fmt == "e4m3":
        vals = np.ascontiguousarray(words).view(ml_dtypes.float8_e4m3fn).astype(np.float64)
    else:
        nib = np.empty((g, p, n, 4), np.uint8)
        nib[..., 0::2] = words & 0xF
        nib[..., 1::2] = words >> 4
        vals = E2M1[nib]
    vals = vals * np.repeat(np.exp2(scales.astype(np.float64) - 127.0), 8, axis=1)[..., None]
    return vals.transpose(0, 1, 3, 2).reshape(g * 512, n)

def pack4(w):
    words, scales = pack_weight(w, "e2m1")
    return words.reshape(words.shape[0], 128, -1), scales


def unpack4(words, scales):
    return unpack_weight(words.reshape(words.shape[0], 128, -1, 2), scales, "e2m1")


def kspread(k):
    return np.exp2(np.repeat(np.random.randint(-6, 7, k // 32), 32).astype(np.float64))


B, S, D, NH, NKV, HD, QB = 1, 128, 8192, 16, 4, 128, 512
Q_DIM = NH * HD
KV_DIM = NKV * HD


def rot(t, f0, f1):
    tp = t.reshape(t.shape[:-1] + (HD // 2, 2))
    t0, t1 = tp[..., 0], tp[..., 1]
    row1 = t0 * f0 + t1 * f1
    row0 = t0 * f1 - t1 * f0
    return np.stack([row0, row1], axis=-1).reshape(t.shape)


def setup_inputs():
    s = kspread(D)
    x = np.random.standard_normal((B, S, D)) * s
    x_words, x_scales = pack4(np.ascontiguousarray(x.reshape(B * S, D).T))
    freqs_cis = bf(np.random.standard_normal((S, HD)))
    w = np.random.standard_normal((Q_DIM + 2 * KV_DIM, D)) / np.sqrt(D) / s
    words, scales = pack4(np.ascontiguousarray(w.T))
    return {"x_words": x_words,
            "x_scales": x_scales,
            "freqs_cis": freqs_cis,
            "Wqkv_words": words,
            "Wqkv_scales": scales}


def reference(x_words, x_scales, freqs_cis, Wqkv_words, Wqkv_scales):
    xqkv = unpack4(x_words, x_scales).T.reshape(B, S, D) @ unpack4(Wqkv_words, Wqkv_scales)
    xq = xqkv[..., :Q_DIM].reshape(B, S, NH, HD)
    xk = xqkv[..., Q_DIM:Q_DIM + KV_DIM].reshape(B, S, NKV, HD)
    xv = xqkv[..., Q_DIM + KV_DIM:].reshape(B, S, NKV, HD)
    f = f64(freqs_cis).reshape(S, 1, HD // 2, 2)
    f0, f1 = f[..., 0], f[..., 1]
    q_rot = rot(xq, f0, f1).transpose(0, 2, 1, 3)
    k_rot = rot(xk, f0, f1).transpose(0, 2, 1, 3)
    v = xv.transpose(0, 2, 1, 3)
    return q_rot, k_rot, v

@@ -1,0 +1,150 @@
+from contextlib import ExitStack
+
+import concourse.mybir as mybir
+
+FLOPS = 2 * 128 * 8192 * 3072
+
+F32 = mybir.dt.float32
+BF16 = mybir.dt.bfloat16
+I32 = mybir.dt.int32
+U8 = mybir.dt.uint8
+FP4X4 = mybir.dt.float4_e2m1fn_x4
+ALU = mybir.AluOpType
+
+P = 128
+PASSES = 16
+COLS = 3072
+NB = 512
+BANKS = COLS // NB
+ROPE_BANKS = 5
+GROUP = 4
+WHOLE = 12
+
+
+def tile_rlaattention_pa_kernel(
+    tc, x_words, x_scales, freqs_cis, Wqkv_words, Wqkv_scales, out_0, out_1, out_2
+):
+    nc = tc.nc
+    with ExitStack() as ctx:
+        keep = ctx.enter_context(tc.tile_pool(name="keep", bufs=1))
+        psum = ctx.enter_context(tc.psum_pool(name="psum", bufs=1))
+        ctx.enter_context(tc.manual_schedule())
+
+        xw = keep.tile([P, PASSES, 256], U8, name="xw", align_bytes=64)
+        xs = keep.tile([P, PASSES, P], U8, name="xs", align_bytes=64)
+        fq = keep.tile([P, 64, 2], BF16, name="fq")
+        fa = keep.tile([P, 64, 2], F32, name="fa")
+        fb = keep.tile([P, 64, 2], F32, name="fb")
+        ws = [
+            keep.tile([P, GROUP, COLS], U8, name="ws%d" % i, align_bytes=64)
+            for i in range(PASSES // GROUP)
+        ]
+        wc = [
+            keep.tile([P, 2 * COLS], U8, name="wc%d" % g, align_bytes=64)
+            for g in range(WHOLE)
+        ]
+        wf = [
+            keep.tile([P, PASSES - WHOLE, 2 * NB], U8, name="wf%d" % b, align_bytes=64)
+            for b in range(BANKS - 1)
+        ]
+        wl = [
+            keep.tile([P, 2 * NB], U8, name="wl%d" % g, align_bytes=64)
+            for g in range(WHOLE, PASSES)
+        ]
+        acc = [psum.tile([P, NB], F32, name="acc%d" % b) for b in range(BANKS)]
+
+        nc.scalar.dma_start(out=fq[:], in_=freqs_cis.rearrange("s (j e) -> s j e", e=2))
+        nc.sync.dma_start(
+            out=xw[:].bitcast(I32), in_=x_words.rearrange("g p b -> p g b").bitcast(I32)
+        )
+        nc.vector.memset(xs[:].bitcast(I32), 0)
+        for t in ws:
+            nc.vector.memset(t[:].bitcast(I32), 0)
+
+        def load_scales(planes, dram, g0, g1):
+            for r in range(4):
+                nc.sync.dma_start(
+                    out=planes[r:P:32, :, :].bitcast(I32),
+                    in_=dram[g0:g1, r:16:4, :].rearrange("g q n -> q g n").bitcast(I32),
+                )
+
+        def load_whole(g):
+            nc.sync.dma_start(out=wc[g][:].bitcast(I32), in_=Wqkv_words[g].bitcast(I32))
+
+        load_scales(xs, x_scales, 0, PASSES)
+        load_scales(ws[0], Wqkv_scales, 0, 4)
+        load_scales(ws[1], Wqkv_scales, 4, 8)
+        for g in range(0, 8):
+            load_whole(g)
+        load_scales(ws[2], Wqkv_scales, 8, 12)
+        load_scales(ws[3], Wqkv_scales, 12, 16)
+        for g in range(8, WHOLE):
+            load_whole(g)
+        for b in range(BANKS - 1):
+            nc.sync.dma_start(
+                out=wf[b][:].bitcast(I32),
+                in_=Wqkv_words[WHOLE:PASSES, :, 2 * NB * b : 2 * NB * (b + 1)]
+                .rearrange("g p c -> p g c")
+                .bitcast(I32),
+            )
+        for g in range(WHOLE, PASSES):
+            nc.sync.dma_start(
+                out=wl[g - WHOLE][:].bitcast(I32),
+                in_=Wqkv_words[g, :, 2 * NB * (BANKS - 1) : 2 * NB * BANKS].bitcast(I32),
+            )
+
+        nc.scalar.copy(out=fa[:], in_=fq[:, :, 1:2].to_broadcast([P, 64, 2]))
+        nc.scalar.copy(out=fb[:, :, 0:1], in_=fq[:, :, 0:1])
+        nc.scalar.mul(out=fb[:, :, 1:2], in_=fq[:, :, 0:1], mul=-1.0)
+        fa_h = fa[:].rearrange("p j e -> p (j e)").unsqueeze(1).to_broadcast([P, 4, P])
+        fb_h = fb[:].rearrange("p j e -> p (j e)").unsqueeze(1).to_broadcast([P, 4, P])
+
+        def mm(g, b, codes):
+            nc.tensor.matmul_mx(
+                out=acc[b][:],
+                lhsT=xw[:, g, :].bitcast(FP4X4),
+                lhsT_scale=xs[:, g, :],
+                rhs=codes.bitcast(FP4X4),
+                rhs_scale=ws[g // GROUP][:, g % GROUP, NB * b : NB * (b + 1)],
+                start=(g == 0),
+                stop=(g == PASSES - 1),
+            )
+
+        for g in range(WHOLE):
+            for b in range(BANKS):
+                mm(g, b, wc[g][:, 2 * NB * b : 2 * NB * (b + 1)])
+
+        dst = [out_0[0, 4 * b : 4 * b + 4].rearrange("h s d -> s h d") for b in range(4)]
+        dst.append(out_1[0].rearrange("h s d -> s h d"))
+        dst.append(out_2[0].rearrange("h s d -> s h d"))
+
+        pa = [keep.tile([P, NB], F32, name="pa%d" % b) for b in range(ROPE_BANKS)]
+        qb = [keep.tile([P, NB], F32, name="qb%d" % b) for b in range(ROPE_BANKS)]
+        ot = [keep.tile([P, NB], F32, name="ot%d" % b) for b in range(BANKS)]
+
+        def finish(b, queue):
+            nc.vector.tensor_tensor(
+                out=ot[b][:].rearrange("p (j e) -> p j e", e=2),
+                in0=pa[b][:].rearrange("p (j e) -> p j e", e=2),
+                in1=qb[b][:].rearrange("p (j e) -> p j e", e=2)[:, :, ::-1],
+                op=ALU.add,
+            )
+            queue.dma_start(out=dst[b], in_=ot[b][:].rearrange("p (h d) -> p h d", h=4))
+
+        for b in range(BANKS):
+            for g in range(WHOLE, PASSES):
+                mm(g, b, wf[b][:, g - WHOLE, :] if b < BANKS - 1 else wl[g - WHOLE][:])
+            if b < ROPE_BANKS:
+                u = acc[b][:].rearrange("p (h d) -> p h d", h=4)
+                nc.vector.tensor_tensor(
+                    out=pa[b][:].rearrange("p (h d) -> p h d", h=4), in0=u, in1=fa_h, op=ALU.mult
+                )
+                nc.vector.tensor_tensor(
+                    out=qb[b][:].rearrange("p (h d) -> p h d", h=4), in0=u, in1=fb_h, op=ALU.mult
+                )
+                if b > 0:
+                    finish(b - 1, nc.scalar)
+            else:
+                nc.scalar.copy(out=ot[b][:], in_=acc[b][:])
+                nc.scalar.dma_start(out=dst[b], in_=ot[b][:].rearrange("p (h d) -> p h d", h=4))
+                finish(ROPE_BANKS - 1, nc.sync)

@@ -17,8 +17,9 @@ COLS = 3072
 NB = 512
 BANKS = COLS // NB
 ROPE_BANKS = 5
-GROUP = 4
-WHOLE = 12
+PLANE_GROUPS = ((0, 4), (4, 8), (8, 12), (12, 14), (14, 16))
+V_ALONE = 10
+BY_BANK = 13
 
 
 def tile_rlaattention_pa_kernel(
@@ -36,20 +37,25 @@ def tile_rlaattention_pa_kernel(
         fa = keep.tile([P, 64, 2], F32, name="fa")
         fb = keep.tile([P, 64, 2], F32, name="fb")
         ws = [
-            keep.tile([P, GROUP, COLS], U8, name="ws%d" % i, align_bytes=64)
-            for i in range(PASSES // GROUP)
+            keep.tile([P, g1 - g0, COLS], U8, name="ws%d" % g0, align_bytes=64)
+            for g0, g1 in PLANE_GROUPS
         ]
         wc = [
-            keep.tile([P, 2 * COLS], U8, name="wc%d" % g, align_bytes=64)
-            for g in range(WHOLE)
+            keep.tile(
+                [P, 2 * NB * (BANKS if g < V_ALONE else ROPE_BANKS)],
+                U8,
+                name="wc%d" % g,
+                align_bytes=64,
+            )
+            for g in range(BY_BANK)
         ]
         wf = [
-            keep.tile([P, PASSES - WHOLE, 2 * NB], U8, name="wf%d" % b, align_bytes=64)
-            for b in range(BANKS - 1)
+            keep.tile([P, PASSES - BY_BANK, 2 * NB], U8, name="wf%d" % b, align_bytes=64)
+            for b in range(ROPE_BANKS)
         ]
-        wl = [
-            keep.tile([P, 2 * NB], U8, name="wl%d" % g, align_bytes=64)
-            for g in range(WHOLE, PASSES)
+        wv = [
+            keep.tile([P, 2 * NB], U8, name="wv%d" % g, align_bytes=64)
+            for g in range(V_ALONE, PASSES)
         ]
         acc = [psum.tile([P, NB], F32, name="acc%d" % b) for b in range(BANKS)]
 
@@ -68,29 +74,25 @@ def tile_rlaattention_pa_kernel(
                     in_=dram[g0:g1, r:16:4, :].rearrange("g q n -> q g n").bitcast(I32),
                 )
 
-        def load_whole(g):
-            nc.sync.dma_start(out=wc[g][:].bitcast(I32), in_=Wqkv_words[g].bitcast(I32))
-
         load_scales(xs, x_scales, 0, PASSES)
-        load_scales(ws[0], Wqkv_scales, 0, 4)
-        load_scales(ws[1], Wqkv_scales, 4, 8)
-        for g in range(0, 8):
-            load_whole(g)
-        load_scales(ws[2], Wqkv_scales, 8, 12)
-        load_scales(ws[3], Wqkv_scales, 12, 16)
-        for g in range(8, WHOLE):
-            load_whole(g)
-        for b in range(BANKS - 1):
+        for t, (g0, g1) in zip(ws, PLANE_GROUPS):
+            load_scales(t, Wqkv_scales, g0, g1)
+        for g in range(BY_BANK):
+            width = 2 * NB * (BANKS if g < V_ALONE else ROPE_BANKS)
+            nc.sync.dma_start(
+                out=wc[g][:].bitcast(I32), in_=Wqkv_words[g, :, 0:width].bitcast(I32)
+            )
+        for b in range(ROPE_BANKS):
             nc.sync.dma_start(
                 out=wf[b][:].bitcast(I32),
-                in_=Wqkv_words[WHOLE:PASSES, :, 2 * NB * b : 2 * NB * (b + 1)]
+                in_=Wqkv_words[BY_BANK:PASSES, :, 2 * NB * b : 2 * NB * (b + 1)]
                 .rearrange("g p c -> p g c")
                 .bitcast(I32),
             )
-        for g in range(WHOLE, PASSES):
+        for g in range(V_ALONE, PASSES):
             nc.sync.dma_start(
-                out=wl[g - WHOLE][:].bitcast(I32),
-                in_=Wqkv_words[g, :, 2 * NB * (BANKS - 1) : 2 * NB * BANKS].bitcast(I32),
+                out=wv[g - V_ALONE][:].bitcast(I32),
+                in_=Wqkv_words[g, :, 2 * NB * ROPE_BANKS : 2 * NB * BANKS].bitcast(I32),
             )
 
         nc.scalar.copy(out=fa[:], in_=fq[:, :, 1:2].to_broadcast([P, 64, 2]))
@@ -99,19 +101,24 @@ def tile_rlaattention_pa_kernel(
         fa_h = fa[:].rearrange("p j e -> p (j e)").unsqueeze(1).to_broadcast([P, 4, P])
         fb_h = fb[:].rearrange("p j e -> p (j e)").unsqueeze(1).to_broadcast([P, 4, P])
 
+        plane_of = {}
+        for t, (g0, g1) in zip(ws, PLANE_GROUPS):
+            for g in range(g0, g1):
+                plane_of[g] = t[:, g - g0, :]
+
         def mm(g, b, codes):
             nc.tensor.matmul_mx(
                 out=acc[b][:],
                 lhsT=xw[:, g, :].bitcast(FP4X4),
                 lhsT_scale=xs[:, g, :],
                 rhs=codes.bitcast(FP4X4),
-                rhs_scale=ws[g // GROUP][:, g % GROUP, NB * b : NB * (b + 1)],
+                rhs_scale=plane_of[g][:, NB * b : NB * (b + 1)],
                 start=(g == 0),
                 stop=(g == PASSES - 1),
             )
 
-        for g in range(WHOLE):
-            for b in range(BANKS):
+        for g in range(BY_BANK):
+            for b in range(BANKS if g < V_ALONE else ROPE_BANKS):
                 mm(g, b, wc[g][:, 2 * NB * b : 2 * NB * (b + 1)])
 
         dst = [out_0[0, 4 * b : 4 * b + 4].rearrange("h s d -> s h d") for b in range(4)]
@@ -131,20 +138,22 @@ def tile_rlaattention_pa_kernel(
             )
             queue.dma_start(out=dst[b], in_=ot[b][:].rearrange("p (h d) -> p h d", h=4))
 
-        for b in range(BANKS):
-            for g in range(WHOLE, PASSES):
-                mm(g, b, wf[b][:, g - WHOLE, :] if b < BANKS - 1 else wl[g - WHOLE][:])
-            if b < ROPE_BANKS:
-                u = acc[b][:].rearrange("p (h d) -> p h d", h=4)
-                nc.vector.tensor_tensor(
-                    out=pa[b][:].rearrange("p (h d) -> p h d", h=4), in0=u, in1=fa_h, op=ALU.mult
-                )
-                nc.vector.tensor_tensor(
-                    out=qb[b][:].rearrange("p (h d) -> p h d", h=4), in0=u, in1=fb_h, op=ALU.mult
-                )
-                if b > 0:
-                    finish(b - 1, nc.scalar)
-            else:
-                nc.scalar.copy(out=ot[b][:], in_=acc[b][:])
-                nc.scalar.dma_start(out=dst[b], in_=ot[b][:].rearrange("p (h d) -> p h d", h=4))
-                finish(ROPE_BANKS - 1, nc.sync)
+        for b in range(ROPE_BANKS):
+            for g in range(BY_BANK, PASSES):
+                mm(g, b, wf[b][:, g - BY_BANK, :])
+            u = acc[b][:].rearrange("p (h d) -> p h d", h=4)
+            nc.vector.tensor_tensor(
+                out=pa[b][:].rearrange("p (h d) -> p h d", h=4), in0=u, in1=fa_h, op=ALU.mult
+            )
+            nc.vector.tensor_tensor(
+                out=qb[b][:].rearrange("p (h d) -> p h d", h=4), in0=u, in1=fb_h, op=ALU.mult
+            )
+            if b > 0:
+                finish(b - 1, nc.scalar)
+        finish(ROPE_BANKS - 1, nc.sync)
+
+        v = BANKS - 1
+        for g in range(V_ALONE, PASSES):
+            mm(g, v, wv[g - V_ALONE][:])
+        nc.scalar.copy(out=ot[v][:], in_=acc[v][:])
+        nc.scalar.dma_start(out=dst[v], in_=ot[v][:].rearrange("p (h d) -> p h d", h=4))

@@ -18,8 +18,11 @@ NB = 512
 BANKS = COLS // NB
 ROPE_BANKS = 5
 PLANE_GROUPS = ((0, 4), (4, 8), (8, 12), (12, 14), (14, 16))
-V_ALONE = 10
+V_ALONE = 12
 BY_BANK = 13
+RANGES = ((0, 2), (2, 4), (4, 5))
+V0 = NB * ROPE_BANKS
+V_PARTS = ((V0, 256), (V0 + 256, 128), (V0 + 384, 128))
 
 
 def tile_rlaattention_pa_kernel(
@@ -42,22 +45,25 @@ def tile_rlaattention_pa_kernel(
         ]
         wc = [
             keep.tile(
-                [P, 2 * NB * (BANKS if g < V_ALONE else ROPE_BANKS)],
-                U8,
-                name="wc%d" % g,
-                align_bytes=64,
+                [P, 2 * (COLS if g < V_ALONE else V0)], U8, name="wc%d" % g, align_bytes=64
             )
             for g in range(BY_BANK)
         ]
         wf = [
-            keep.tile([P, PASSES - BY_BANK, 2 * NB], U8, name="wf%d" % b, align_bytes=64)
-            for b in range(ROPE_BANKS)
+            keep.tile(
+                [P, PASSES - BY_BANK, 2 * NB * (b1 - b0)], U8, name="wf%d" % b0, align_bytes=64
+            )
+            for b0, b1 in RANGES
         ]
         wv = [
             keep.tile([P, 2 * NB], U8, name="wv%d" % g, align_bytes=64)
-            for g in range(V_ALONE, PASSES)
+            for g in range(V_ALONE, PASSES - 1)
         ]
-        acc = [psum.tile([P, NB], F32, name="acc%d" % b) for b in range(BANKS)]
+        wz = [
+            keep.tile([P, 2 * n], U8, name="wz%d" % c0, align_bytes=64) for c0, n in V_PARTS
+        ]
+        acc = [psum.tile([P, NB], F32, name="acc%d" % b) for b in range(ROPE_BANKS)]
+        vac = [psum.tile([P, n], F32, name="vac%d" % c0) for c0, n in V_PARTS]
 
         nc.scalar.dma_start(out=fq[:], in_=freqs_cis.rearrange("s (j e) -> s j e", e=2))
         nc.sync.dma_start(
@@ -78,82 +84,102 @@ def tile_rlaattention_pa_kernel(
         for t, (g0, g1) in zip(ws, PLANE_GROUPS):
             load_scales(t, Wqkv_scales, g0, g1)
         for g in range(BY_BANK):
-            width = 2 * NB * (BANKS if g < V_ALONE else ROPE_BANKS)
+            width = 2 * (COLS if g < V_ALONE else V0)
             nc.sync.dma_start(
                 out=wc[g][:].bitcast(I32), in_=Wqkv_words[g, :, 0:width].bitcast(I32)
             )
-        for b in range(ROPE_BANKS):
+        for t, (b0, b1) in zip(wf, RANGES):
             nc.sync.dma_start(
-                out=wf[b][:].bitcast(I32),
-                in_=Wqkv_words[BY_BANK:PASSES, :, 2 * NB * b : 2 * NB * (b + 1)]
+                out=t[:].bitcast(I32),
+                in_=Wqkv_words[BY_BANK:PASSES, :, 2 * NB * b0 : 2 * NB * b1]
                 .rearrange("g p c -> p g c")
                 .bitcast(I32),
             )
-        for g in range(V_ALONE, PASSES):
+        for g in range(V_ALONE, PASSES - 1):
             nc.sync.dma_start(
                 out=wv[g - V_ALONE][:].bitcast(I32),
-                in_=Wqkv_words[g, :, 2 * NB * ROPE_BANKS : 2 * NB * BANKS].bitcast(I32),
+                in_=Wqkv_words[g, :, 2 * V0 : 2 * COLS].bitcast(I32),
+            )
+        for t, (c0, n) in zip(wz, V_PARTS):
+            nc.sync.dma_start(
+                out=t[:].bitcast(I32),
+                in_=Wqkv_words[PASSES - 1, :, 2 * c0 : 2 * (c0 + n)].bitcast(I32),
             )
 
         nc.scalar.copy(out=fa[:], in_=fq[:, :, 1:2].to_broadcast([P, 64, 2]))
-        nc.scalar.copy(out=fb[:, :, 0:1], in_=fq[:, :, 0:1])
-        nc.scalar.mul(out=fb[:, :, 1:2], in_=fq[:, :, 0:1], mul=-1.0)
-        fa_h = fa[:].rearrange("p j e -> p (j e)").unsqueeze(1).to_broadcast([P, 4, P])
-        fb_h = fb[:].rearrange("p j e -> p (j e)").unsqueeze(1).to_broadcast([P, 4, P])
+        nc.scalar.mul(out=fb[:, :, 0:1], in_=fq[:, :, 0:1], mul=-1.0)
+        nc.scalar.copy(out=fb[:, :, 1:2], in_=fq[:, :, 0:1])
+        fa_h = fa[:].unsqueeze(1).to_broadcast([P, 4, 64, 2])
+        fb_h = fb[:].unsqueeze(1).to_broadcast([P, 4, 64, 2])
 
         plane_of = {}
         for t, (g0, g1) in zip(ws, PLANE_GROUPS):
             for g in range(g0, g1):
                 plane_of[g] = t[:, g - g0, :]
 
-        def mm(g, b, codes):
+        def mm(out, g, c0, n, codes):
             nc.tensor.matmul_mx(
-                out=acc[b][:],
+                out=out,
                 lhsT=xw[:, g, :].bitcast(FP4X4),
                 lhsT_scale=xs[:, g, :],
                 rhs=codes.bitcast(FP4X4),
-                rhs_scale=plane_of[g][:, NB * b : NB * (b + 1)],
+                rhs_scale=plane_of[g][:, c0 : c0 + n],
                 start=(g == 0),
                 stop=(g == PASSES - 1),
             )
 
         for g in range(BY_BANK):
-            for b in range(BANKS if g < V_ALONE else ROPE_BANKS):
-                mm(g, b, wc[g][:, 2 * NB * b : 2 * NB * (b + 1)])
+            for b in range(ROPE_BANKS):
+                mm(acc[b][:], g, NB * b, NB, wc[g][:, 2 * NB * b : 2 * NB * (b + 1)])
+            if g < V_ALONE:
+                for a, (c0, n) in zip(vac, V_PARTS):
+                    mm(a[:], g, c0, n, wc[g][:, 2 * c0 : 2 * (c0 + n)])
 
         dst = [out_0[0, 4 * b : 4 * b + 4].rearrange("h s d -> s h d") for b in range(4)]
         dst.append(out_1[0].rearrange("h s d -> s h d"))
-        dst.append(out_2[0].rearrange("h s d -> s h d"))
+        v_dst = out_2[0].rearrange("h s d -> s h d")
 
         pa = [keep.tile([P, NB], F32, name="pa%d" % b) for b in range(ROPE_BANKS)]
         qb = [keep.tile([P, NB], F32, name="qb%d" % b) for b in range(ROPE_BANKS)]
-        ot = [keep.tile([P, NB], F32, name="ot%d" % b) for b in range(BANKS)]
+        ot = [keep.tile([P, NB], F32, name="ot%d" % b) for b in range(ROPE_BANKS)]
+        vt = [keep.tile([P, n], F32, name="vt%d" % c0) for c0, n in V_PARTS]
 
-        def finish(b, queue):
-            nc.vector.tensor_tensor(
-                out=ot[b][:].rearrange("p (j e) -> p j e", e=2),
-                in0=pa[b][:].rearrange("p (j e) -> p j e", e=2),
-                in1=qb[b][:].rearrange("p (j e) -> p j e", e=2)[:, :, ::-1],
-                op=ALU.add,
-            )
-            queue.dma_start(out=dst[b], in_=ot[b][:].rearrange("p (h d) -> p h d", h=4))
+        def pairs(ap):
+            return ap.rearrange("p (h j e) -> p h j e", h=4, e=2)
 
-        for b in range(ROPE_BANKS):
-            for g in range(BY_BANK, PASSES):
-                mm(g, b, wf[b][:, g - BY_BANK, :])
-            u = acc[b][:].rearrange("p (h d) -> p h d", h=4)
-            nc.vector.tensor_tensor(
-                out=pa[b][:].rearrange("p (h d) -> p h d", h=4), in0=u, in1=fa_h, op=ALU.mult
-            )
-            nc.vector.tensor_tensor(
-                out=qb[b][:].rearrange("p (h d) -> p h d", h=4), in0=u, in1=fb_h, op=ALU.mult
-            )
-            if b > 0:
-                finish(b - 1, nc.scalar)
-        finish(ROPE_BANKS - 1, nc.sync)
+        for t, (b0, b1) in zip(wf, RANGES):
+            for b in range(b0, b1):
+                for g in range(BY_BANK, PASSES):
+                    mm(
+                        acc[b][:],
+                        g,
+                        NB * b,
+                        NB,
+                        t[:, g - BY_BANK, 2 * NB * (b - b0) : 2 * NB * (b - b0 + 1)],
+                    )
+                u = pairs(acc[b][:])
+                nc.vector.tensor_tensor(out=pairs(pa[b][:]), in0=u, in1=fa_h, op=ALU.mult)
+                nc.vector.tensor_tensor(
+                    out=pairs(qb[b][:]), in0=u[:, :, :, ::-1], in1=fb_h, op=ALU.mult
+                )
+                adder = nc.gpsimd if b < ROPE_BANKS - 1 else nc.vector
+                adder.tensor_tensor(out=ot[b][:], in0=pa[b][:], in1=qb[b][:], op=ALU.add)
+                queue = nc.scalar if b < ROPE_BANKS - 1 else nc.sync
+                queue.dma_start(out=dst[b], in_=ot[b][:].rearrange("p (h d) -> p h d", h=4))
 
-        v = BANKS - 1
-        for g in range(V_ALONE, PASSES):
-            mm(g, v, wv[g - V_ALONE][:])
-        nc.scalar.copy(out=ot[v][:], in_=acc[v][:])
-        nc.scalar.dma_start(out=dst[v], in_=ot[v][:].rearrange("p (h d) -> p h d", h=4))
+        for g in range(V_ALONE, PASSES - 1):
+            for a, (c0, n) in zip(vac, V_PARTS):
+                mm(a[:], g, c0, n, wv[g - V_ALONE][:, 2 * (c0 - V0) : 2 * (c0 - V0 + n)])
+        for i, (c0, n) in enumerate(V_PARTS):
+            mm(vac[i][:], PASSES - 1, c0, n, wz[i][:])
+            h0 = (c0 - V0) // P
+            if i == 0:
+                nc.scalar.copy(out=vt[i][:], in_=vac[i][:])
+                queue = nc.scalar
+            else:
+                nc.vector.tensor_copy(out=vt[i][:], in_=vac[i][:])
+                queue = nc.sync
+            queue.dma_start(
+                out=v_dst[:, h0 : h0 + n // P, :],
+                in_=vt[i][:].rearrange("p (h d) -> p h d", d=P),
+            )

@@ -17,7 +17,8 @@ COLS = 3072
 NB = 512
 BANKS = COLS // NB
 ROPE_BANKS = 5
-PLANE_GROUPS = ((0, 4), (4, 8), (8, 12), (12, 14), (14, 16))
+PLANE_GROUPS = ((0, 2), (2, 4), (4, 8), (8, 12), (12, 14), (14, 16))
+EARLY = 4
 V_ALONE = 12
 BY_BANK = 13
 RANGES = ((0, 2), (2, 4), (4, 5))
@@ -81,13 +82,23 @@ def tile_rlaattention_pa_kernel(
                 )
 
         load_scales(xs, x_scales, 0, PASSES)
-        for t, (g0, g1) in zip(ws, PLANE_GROUPS):
-            load_scales(t, Wqkv_scales, g0, g1)
-        for g in range(BY_BANK):
+
+        def load_rows(g):
             width = 2 * (COLS if g < V_ALONE else V0)
             nc.sync.dma_start(
                 out=wc[g][:].bitcast(I32), in_=Wqkv_words[g, :, 0:width].bitcast(I32)
             )
+
+        for t, (g0, g1) in zip(ws, PLANE_GROUPS):
+            if g1 <= EARLY:
+                load_scales(t, Wqkv_scales, g0, g1)
+        for g in range(EARLY):
+            load_rows(g)
+        for t, (g0, g1) in zip(ws, PLANE_GROUPS):
+            if g0 >= EARLY:
+                load_scales(t, Wqkv_scales, g0, g1)
+        for g in range(EARLY, BY_BANK):
+            load_rows(g)
         for t, (b0, b1) in zip(wf, RANGES):
             nc.sync.dma_start(
                 out=t[:].bitcast(I32),

@@ -17,8 +17,7 @@ COLS = 3072
 NB = 512
 BANKS = COLS // NB
 ROPE_BANKS = 5
-PLANE_GROUPS = ((0, 2), (2, 4), (4, 8), (8, 12), (12, 14), (14, 16))
-EARLY = 4
+PLANE_GROUPS = ((0, 2), (2, 4), (4, 8), (8, 12), (12, 16))
 V_ALONE = 12
 BY_BANK = 13
 RANGES = ((0, 2), (2, 4), (4, 5))
@@ -74,14 +73,14 @@ def tile_rlaattention_pa_kernel(
         for t in ws:
             nc.vector.memset(t[:].bitcast(I32), 0)
 
-        def load_scales(planes, dram, g0, g1):
+        def load_scales(queue, view, planes, dram, g0, g1):
             for r in range(4):
-                nc.sync.dma_start(
-                    out=planes[r:P:32, :, :].bitcast(I32),
-                    in_=dram[g0:g1, r:16:4, :].rearrange("g q n -> q g n").bitcast(I32),
+                queue.dma_start(
+                    out=planes[r:P:32, :, :].bitcast(view),
+                    in_=dram[g0:g1, r:16:4, :].rearrange("g q n -> q g n").bitcast(view),
                 )
 
-        load_scales(xs, x_scales, 0, PASSES)
+        load_scales(nc.sync, I32, xs, x_scales, 0, PASSES)
 
         def load_rows(g):
             width = 2 * (COLS if g < V_ALONE else V0)
@@ -90,14 +89,8 @@ def tile_rlaattention_pa_kernel(
             )
 
         for t, (g0, g1) in zip(ws, PLANE_GROUPS):
-            if g1 <= EARLY:
-                load_scales(t, Wqkv_scales, g0, g1)
-        for g in range(EARLY):
-            load_rows(g)
-        for t, (g0, g1) in zip(ws, PLANE_GROUPS):
-            if g0 >= EARLY:
-                load_scales(t, Wqkv_scales, g0, g1)
-        for g in range(EARLY, BY_BANK):
+            load_scales(nc.gpsimd, F32, t, Wqkv_scales, g0, g1)
+        for g in range(BY_BANK):
             load_rows(g)
         for t, (b0, b1) in zip(wf, RANGES):
             nc.sync.dma_start(

from contextlib import ExitStack

import concourse.mybir as mybir

FLOPS = 2 * 128 * 8192 * 3072

F32 = mybir.dt.float32
BF16 = mybir.dt.bfloat16
I32 = mybir.dt.int32
U8 = mybir.dt.uint8
FP4X4 = mybir.dt.float4_e2m1fn_x4
ALU = mybir.AluOpType

P = 128
PASSES = 16
COLS = 3072
NB = 512
BANKS = COLS // NB
ROPE_BANKS = 5
PLANE_GROUPS = ((0, 2), (2, 4), (4, 8), (8, 12), (12, 16))
V_ALONE = 12
BY_BANK = 13
RANGES = ((0, 2), (2, 4), (4, 5))
V0 = NB * ROPE_BANKS
V_PARTS = ((V0, 256), (V0 + 256, 128), (V0 + 384, 128))


def tile_rlaattention_pa_kernel(
    tc, x_words, x_scales, freqs_cis, Wqkv_words, Wqkv_scales, out_0, out_1, out_2
):
    nc = tc.nc
    with ExitStack() as ctx:
        keep = ctx.enter_context(tc.tile_pool(name="keep", bufs=1))
        psum = ctx.enter_context(tc.psum_pool(name="psum", bufs=1))
        ctx.enter_context(tc.manual_schedule())

        xw = keep.tile([P, PASSES, 256], U8, name="xw", align_bytes=64)
        xs = keep.tile([P, PASSES, P], U8, name="xs", align_bytes=64)
        fq = keep.tile([P, 64, 2], BF16, name="fq")
        fa = keep.tile([P, 64, 2], F32, name="fa")
        fb = keep.tile([P, 64, 2], F32, name="fb")
        ws = [
            keep.tile([P, g1 - g0, COLS], U8, name="ws%d" % g0, align_bytes=64)
            for g0, g1 in PLANE_GROUPS
        ]
        wc = [
            keep.tile(
                [P, 2 * (COLS if g < V_ALONE else V0)], U8, name="wc%d" % g, align_bytes=64
            )
            for g in range(BY_BANK)
        ]
        wf = [
            keep.tile(
                [P, PASSES - BY_BANK, 2 * NB * (b1 - b0)], U8, name="wf%d" % b0, align_bytes=64
            )
            for b0, b1 in RANGES
        ]
        wv = [
            keep.tile([P, 2 * NB], U8, name="wv%d" % g, align_bytes=64)
            for g in range(V_ALONE, PASSES - 1)
        ]
        wz = [
            keep.tile([P, 2 * n], U8, name="wz%d" % c0, align_bytes=64) for c0, n in V_PARTS
        ]
        acc = [psum.tile([P, NB], F32, name="acc%d" % b) for b in range(ROPE_BANKS)]
        vac = [psum.tile([P, n], F32, name="vac%d" % c0) for c0, n in V_PARTS]

        nc.scalar.dma_start(out=fq[:], in_=freqs_cis.rearrange("s (j e) -> s j e", e=2))
        nc.sync.dma_start(
            out=xw[:].bitcast(I32), in_=x_words.rearrange("g p b -> p g b").bitcast(I32)
        )
        nc.vector.memset(xs[:].bitcast(I32), 0)
        for t in ws:
            nc.vector.memset(t[:].bitcast(I32), 0)

        def load_scales(queue, view, planes, dram, g0, g1):
            for r in range(4):
                queue.dma_start(
                    out=planes[r:P:32, :, :].bitcast(view),
                    in_=dram[g0:g1, r:16:4, :].rearrange("g q n -> q g n").bitcast(view),
                )

        load_scales(nc.sync, I32, xs, x_scales, 0, PASSES)

        def load_rows(g):
            width = 2 * (COLS if g < V_ALONE else V0)
            nc.sync.dma_start(
                out=wc[g][:].bitcast(I32), in_=Wqkv_words[g, :, 0:width].bitcast(I32)
            )

        for t, (g0, g1) in zip(ws, PLANE_GROUPS):
            load_scales(nc.gpsimd, F32, t, Wqkv_scales, g0, g1)
        for g in range(BY_BANK):
            load_rows(g)
        for t, (b0, b1) in zip(wf, RANGES):
            nc.sync.dma_start(
                out=t[:].bitcast(I32),
                in_=Wqkv_words[BY_BANK:PASSES, :, 2 * NB * b0 : 2 * NB * b1]
                .rearrange("g p c -> p g c")
                .bitcast(I32),
            )
        for g in range(V_ALONE, PASSES - 1):
            nc.sync.dma_start(
                out=wv[g - V_ALONE][:].bitcast(I32),
                in_=Wqkv_words[g, :, 2 * V0 : 2 * COLS].bitcast(I32),
            )
        for t, (c0, n) in zip(wz, V_PARTS):
            nc.sync.dma_start(
                out=t[:].bitcast(I32),
                in_=Wqkv_words[PASSES - 1, :, 2 * c0 : 2 * (c0 + n)].bitcast(I32),
            )

        nc.scalar.copy(out=fa[:], in_=fq[:, :, 1:2].to_broadcast([P, 64, 2]))
        nc.scalar.mul(out=fb[:, :, 0:1], in_=fq[:, :, 0:1], mul=-1.0)
        nc.scalar.copy(out=fb[:, :, 1:2], in_=fq[:, :, 0:1])
        fa_h = fa[:].unsqueeze(1).to_broadcast([P, 4, 64, 2])
        fb_h = fb[:].unsqueeze(1).to_broadcast([P, 4, 64, 2])

        plane_of = {}
        for t, (g0, g1) in zip(ws, PLANE_GROUPS):
            for g in range(g0, g1):
                plane_of[g] = t[:, g - g0, :]

        def mm(out, g, c0, n, codes):
            nc.tensor.matmul_mx(
                out=out,
                lhsT=xw[:, g, :].bitcast(FP4X4),
                lhsT_scale=xs[:, g, :],
                rhs=codes.bitcast(FP4X4),
                rhs_scale=plane_of[g][:, c0 : c0 + n],
                start=(g == 0),
                stop=(g == PASSES - 1),
            )

        for g in range(BY_BANK):
            for b in range(ROPE_BANKS):
                mm(acc[b][:], g, NB * b, NB, wc[g][:, 2 * NB * b : 2 * NB * (b + 1)])
            if g < V_ALONE:
                for a, (c0, n) in zip(vac, V_PARTS):
                    mm(a[:], g, c0, n, wc[g][:, 2 * c0 : 2 * (c0 + n)])

        dst = [out_0[0, 4 * b : 4 * b + 4].rearrange("h s d -> s h d") for b in range(4)]
        dst.append(out_1[0].rearrange("h s d -> s h d"))
        v_dst = out_2[0].rearrange("h s d -> s h d")

        pa = [keep.tile([P, NB], F32, name="pa%d" % b) for b in range(ROPE_BANKS)]
        qb = [keep.tile([P, NB], F32, name="qb%d" % b) for b in range(ROPE_BANKS)]
        ot = [keep.tile([P, NB], F32, name="ot%d" % b) for b in range(ROPE_BANKS)]
        vt = [keep.tile([P, n], F32, name="vt%d" % c0) for c0, n in V_PARTS]

        def pairs(ap):
            return ap.rearrange("p (h j e) -> p h j e", h=4, e=2)

        for t, (b0, b1) in zip(wf, RANGES):
            for b in range(b0, b1):
                for g in range(BY_BANK, PASSES):
                    mm(
                        acc[b][:],
                        g,
                        NB * b,
                        NB,
                        t[:, g - BY_BANK, 2 * NB * (b - b0) : 2 * NB * (b - b0 + 1)],
                    )
                u = pairs(acc[b][:])
                nc.vector.tensor_tensor(out=pairs(pa[b][:]), in0=u, in1=fa_h, op=ALU.mult)
                nc.vector.tensor_tensor(
                    out=pairs(qb[b][:]), in0=u[:, :, :, ::-1], in1=fb_h, op=ALU.mult
                )
                adder = nc.gpsimd if b < ROPE_BANKS - 1 else nc.vector
                adder.tensor_tensor(out=ot[b][:], in0=pa[b][:], in1=qb[b][:], op=ALU.add)
                queue = nc.scalar if b < ROPE_BANKS - 1 else nc.sync
                queue.dma_start(out=dst[b], in_=ot[b][:].rearrange("p (h d) -> p h d", h=4))

        for g in range(V_ALONE, PASSES - 1):
            for a, (c0, n) in zip(vac, V_PARTS):
                mm(a[:], g, c0, n, wv[g - V_ALONE][:, 2 * (c0 - V0) : 2 * (c0 - V0 + n)])
        for i, (c0, n) in enumerate(V_PARTS):
            mm(vac[i][:], PASSES - 1, c0, n, wz[i][:])
            h0 = (c0 - V0) // P
            if i == 0:
                nc.scalar.copy(out=vt[i][:], in_=vac[i][:])
                queue = nc.scalar
            else:
                nc.vector.tensor_copy(out=vt[i][:], in_=vac[i][:])
                queue = nc.sync
            queue.dma_start(
                out=v_dst[:, h0 : h0 + n // P, :],
                in_=vt[i][:].rearrange("p (h d) -> p h d", d=P),
            )
